import numpy as np
import ml_dtypes


def mxq(x, axis, fmt="e4m3"):
    dtype, down = {"e4m3": (ml_dtypes.float8_e4m3fn, 7), "e5m2": (ml_dtypes.float8_e5m2, 14)}[fmt]
    v = np.moveaxis(np.asarray(x, np.float32).astype(ml_dtypes.bfloat16).astype(np.float64), axis, -1)
    blocks = v.reshape(v.shape[:-1] + (-1, 32))
    amax = np.abs(blocks).max(-1, keepdims=True)
    byte = np.maximum(np.where(amax > 0, np.frexp(amax)[1] - 1 + 127, 0) - down, 1)
    scale = np.exp2(byte - 127.0)
    codes = (blocks / scale).astype(np.float32).astype(dtype).astype(np.float64)
    return np.moveaxis((codes * scale).reshape(v.shape), -1, axis)


WIDE = False


def mx_kscale(k):
    if not WIDE:
        return np.ones(k)
    levels = np.array([10, -10, 5, -5, 0])
    a = np.random.permutation(np.resize(levels, k // 512 * 4)).reshape(k // 512, 4)
    idx = np.arange(k)
    return np.exp2(a[idx // 512, idx % 128 // 32])


BF16 = ml_dtypes.bfloat16


def bf(x):
    return np.asarray(x, np.float32).astype(BF16)


def f64(x):
    return np.asarray(x).astype(np.float64)


B, S, D, H, HD = 1, 512, 2048, 16, 128
E = H * HD
EPS = 1e-5
NEG = -1e9


def get_slopes(n):
    start = 2.0 ** (-2.0 ** (-(np.log2(n) - 3)))
    return np.array([start * start ** i for i in range(n)])


def prior_bias(shape, scale, loc):
    q_pos = np.arange(S, dtype=np.float64)
    k_pos = np.arange(S, dtype=np.float64)
    dist = (k_pos[None, :] - q_pos[:, None])[None, None]
    loc_t = np.exp(loc) - np.exp(-loc)
    z = (dist - loc_t) * np.exp(scale)
    return -(np.abs(z) + EPS) ** shape


def setup_inputs():
    s = mx_kscale(D)
    causal = np.tril(np.ones((S, S), dtype=bool))
    return {"x": bf(np.random.standard_normal((B, S, D)) * s),
            "wv": bf(np.random.standard_normal((D, E)) * 2.0 / np.sqrt(D) / s[:, None]),
            "q": bf(np.random.standard_normal((B, S, H, HD))),
            "k": bf(np.random.standard_normal((B, S, H, HD))),
            "mask": bf(np.where(causal, 0.0, NEG))[None, None],
            "shape": bf(1.0 + 0.1 * np.random.standard_normal((1, H, 1, 1))),
            "scale": bf(np.log(get_slopes(H)).reshape(1, H, 1, 1) + 0.1 * np.random.standard_normal((1, H, 1, 1))),
            "loc": bf(-2.0 + 0.5 * np.random.standard_normal((1, H, 1, 1)))}


def reference(x, wv, q, k, mask, shape, scale, loc):
    v = (mxq(f64(x), 2, "e4m3") @ mxq(f64(wv), 0, "e4m3")).reshape(B, S, H, HD)
    s = f64(q).transpose(0, 2, 1, 3) @ f64(k).transpose(0, 2, 3, 1) / np.sqrt(HD)
    s = s + prior_bias(f64(shape), f64(scale), f64(loc))
    s = s + f64(mask)
    e = np.exp(s - s.max(-1, keepdims=True))
    o = (mxq(e, 3, "e4m3") @ mxq(v.transpose(0, 2, 1, 3), 2, "e4m3")) / e.sum(-1, keepdims=True)
    return o.transpose(0, 2, 1, 3).reshape(B, S, E)

@@ -1,0 +1,282 @@
+from contextlib import ExitStack
+import math
+
+import concourse.mybir as mybir
+from concourse.masks import make_identity
+
+F32 = mybir.dt.float32
+BF16 = mybir.dt.bfloat16
+U32 = mybir.dt.uint32
+U8 = mybir.dt.uint8
+FP8X4 = mybir.dt.float8_e4m3fn_x4
+ACT = mybir.ActivationFunctionType
+ALU = mybir.AluOpType
+AXIS = mybir.AxisListType
+
+P = 128
+S = 512
+D = 2048
+H = 16
+HD = 128
+PACK = 4
+K_PASS = P * PACK
+PASSES = D // K_PASS
+TILES = S // P
+GROUP = 4
+CHUNK = GROUP * HD
+EPS = 1e-5
+INV_SQRT_HD = 1.0 / math.sqrt(HD)
+
+FLOPS = 2 * S * D * H * HD + 2 * (2 * H * S * S * HD)
+
+
+def tile_bayesianattention_pa_kernel(tc, x, wv, q, k, mask, shape, scale, loc, out):
+    nc = tc.nc
+    with ExitStack() as ctx:
+        const = ctx.enter_context(tc.tile_pool(name="const", bufs=1))
+        loads = ctx.enter_context(tc.tile_pool(name="loads", bufs=2))
+        stage = ctx.enter_context(tc.tile_pool(name="stage", bufs=4))
+        work = ctx.enter_context(tc.tile_pool(name="work", bufs=2))
+        psum = ctx.enter_context(tc.psum_pool(name="psum", bufs=2))
+
+        ident_bf = const.tile([P, P], BF16)
+        make_identity(nc, ident_bf[:])
+        ident_f32 = const.tile([P, P], F32)
+        make_identity(nc, ident_f32[:])
+
+        par_bf = const.tile([P, 3, H], BF16)
+        for row, vec in enumerate((scale, loc, shape)):
+            nc.sync.dma_start(
+                out=par_bf[:, row, :],
+                in_=vec.rearrange("a h b c -> (a h b c)").partition_broadcast(P),
+            )
+        mask_diag = const.tile([P, P], BF16)
+        nc.sync.dma_start(out=mask_diag[:], in_=mask[0, 0, 0:P, 0:P])
+
+        exp_loc = const.tile([P, H], F32)
+        exp_neg_loc = const.tile([P, H], F32)
+        eps_h = const.tile([P, H], F32)
+        nc.scalar.activation(out=exp_loc[:], in_=par_bf[:, 1, :], func=ACT.Exp)
+        nc.scalar.activation(out=exp_neg_loc[:], in_=par_bf[:, 1, :], func=ACT.Exp, scale=-1.0)
+        nc.scalar.activation(out=eps_h[:], in_=par_bf[:, 0, :], func=ACT.Exp, scale=-1.0)
+        nc.vector.tensor_scalar_mul(out=eps_h[:], in0=eps_h[:], scalar1=EPS)
+        neg_centre = const.tile([P, H], F32)
+        nc.vector.tensor_sub(out=neg_centre[:], in0=exp_neg_loc[:], in1=exp_loc[:])
+        power = const.tile([P, H], F32)
+        nc.vector.tensor_copy(out=power[:], in_=par_bf[:, 2, :])
+        log_gain = const.tile([P, H], F32)
+        nc.vector.tensor_mul(out=log_gain[:], in0=power[:], in1=par_bf[:, 0, :])
+
+        x_rows = x.rearrange("b (t p) d -> p (b t) d", p=P)
+        x_sb = const.tile([P, TILES, D], BF16)
+        for t in range(TILES):
+            nc.sync.dma_start(out=x_sb[:, t, :], in_=x_rows[:, t, :])
+        x_words = x_sb[:].bitcast(F32)
+        x_codes = const.tile([P, PASSES, S], U32, align_bytes=64)
+        x_scales = const.tile([P, PASSES, S], U8, align_bytes=64)
+        for g in range(PASSES):
+            x_grouped = stage.tile([P, S, PACK], BF16, align_bytes=64)
+            grouped_words = x_grouped[:].bitcast(F32)
+            for half in range(2):
+                xt = psum.tile([P, 2, 2 * P], F32, tag="tp")
+                for u in range(2):
+                    first_word = (K_PASS // 2) * g + P * u
+                    for tt in range(2):
+                        nc.tensor.transpose(
+                            xt[:, u, P * tt : P * (tt + 1)],
+                            x_words[:, 2 * half + tt, first_word : first_word + P],
+                            ident_f32[:],
+                        )
+                nc.vector.tensor_copy(
+                    out=grouped_words[:, 2 * P * half : 2 * P * (half + 1), :],
+                    in_=xt[:].rearrange("p u s -> p s u"),
+                )
+            nc.vector.quantize_mx(
+                out=x_codes[:, g, :].bitcast(FP8X4),
+                scales=x_scales[:, g, :],
+                in_=x_grouped[:].rearrange("p s t -> p (s t)"),
+            )
+
+        dist = const.tile([P, S], F32)
+        nc.gpsimd.iota(
+            dist[:], pattern=[[1, S]], base=-(S - P), channel_multiplier=-1,
+            allow_small_or_imprecise_dtypes=True,
+        )
+        prior = const.tile([P, H, S], F32)
+        for h in range(H):
+            nc.scalar.activation(
+                out=prior[:, h, :], in_=dist[:], func=ACT.Abs, bias=neg_centre[:, h : h + 1]
+            )
+        for h in range(H):
+            nc.scalar.activation(
+                out=prior[:, h, :], in_=prior[:, h, :], func=ACT.Ln, bias=eps_h[:, h : h + 1]
+            )
+        for h in range(H):
+            nc.scalar.activation(
+                out=prior[:, h, :], in_=prior[:, h, :], func=ACT.Exp,
+                scale=power[:, h : h + 1], bias=log_gain[:, h : h + 1],
+            )
+        for c in range(H // GROUP):
+            heads = slice(GROUP * c, GROUP * (c + 1))
+            nc.vector.tensor_tensor(
+                out=prior[:, heads, S - P : S],
+                in0=prior[:, heads, S - P : S],
+                in1=mask_diag[:].unsqueeze(1).to_broadcast([P, GROUP, P]),
+                op=ALU.subtract,
+            )
+
+        e_grouped = [
+            const.tile([P, S, PACK], BF16, align_bytes=64, name="e_grouped%d" % n) for n in range(2)
+        ]
+        for n in range(2):
+            nc.vector.memset(e_grouped[n][:], 0.0)
+
+        wv_rows = wv.rearrange("(r p e) c -> p r e c", p=P, e=2)
+        q_rows = q.rearrange("b (t p) h d -> p (b t) (h d)", p=P)
+        k_rows = k.rearrange("b (t p) h d -> p (b t) (h d)", p=P)
+        out_rows = out.rearrange("b (t p) c -> p (b t) c", p=P)
+
+        for c in range(H // GROUP):
+            cols = slice(CHUNK * c, CHUNK * (c + 1))
+            wv_raw = loads.tile([P, 2 * PASSES, 2, CHUNK], BF16)
+            for e in range(2):
+                nc.sync.dma_start(out=wv_raw[:, :, e, :], in_=wv_rows[:, :, e, cols])
+            q_sb = loads.tile([P, TILES, CHUNK], BF16)
+            nc.sync.dma_start(out=q_sb[:], in_=q_rows[:, :, cols])
+            k_sb = loads.tile([P, TILES, CHUNK], BF16)
+            nc.sync.dma_start(out=k_sb[:], in_=k_rows[:, :, cols])
+
+            wv_codes = work.tile([P, PASSES, CHUNK], U32, align_bytes=64)
+            wv_scales = work.tile([P, PASSES, CHUNK], U8, align_bytes=64)
+            wv_grouped = []
+            for g in range(PASSES):
+                grouped = stage.tile([P, CHUNK, PACK], BF16, align_bytes=64, tag="wv_grouped", name="wv_grouped")
+                four_rows = wv_raw[:, 2 * g : 2 * g + 2, :, :].rearrange("p u e c -> p (u e) c")
+                nc.vector.tensor_copy(
+                    out=grouped[:].rearrange("p (c i) t -> p c t i", i=4),
+                    in_=four_rows.rearrange("p t (c i) -> p c t i", i=4),
+                )
+                wv_grouped.append(grouped)
+            for g in range(PASSES):
+                nc.vector.quantize_mx(
+                    out=wv_codes[:, g, :].bitcast(FP8X4),
+                    scales=wv_scales[:, g, :],
+                    in_=wv_grouped[g][:].rearrange("p c t -> p (c t)"),
+                )
+
+            out_sb = work.tile([P, TILES, CHUNK], F32)
+            for hh in range(GROUP):
+                h = GROUP * c + hh
+                head_cols = slice(HD * hh, HD * (hh + 1))
+
+                v_ps = psum.tile([P, TILES, HD], F32, tag="v", bufs=1)
+                for t in range(TILES):
+                    for g in range(PASSES):
+                        nc.tensor.matmul_mx(
+                            out=v_ps[:, t, :],
+                            lhsT=x_codes[:, g, P * t : P * (t + 1)].bitcast(FP8X4),
+                            lhsT_scale=x_scales[:, g, P * t : P * (t + 1)],
+                            rhs=wv_codes[:, g, head_cols].bitcast(FP8X4),
+                            rhs_scale=wv_scales[:, g, head_cols],
+                            start=(g == 0),
+                            stop=(g == PASSES - 1),
+                        )
+                v_grouped = work.tile([P, HD, PACK], BF16, align_bytes=64)
+                nc.scalar.copy(out=v_grouped[:], in_=v_ps[:].rearrange("p t d -> p d t"))
+                v_codes = work.tile([P, HD], U32, align_bytes=64)
+                v_scales = work.tile([P, HD], U8, align_bytes=64)
+                nc.vector.quantize_mx(
+                    out=v_codes[:].bitcast(FP8X4),
+                    scales=v_scales[:],
+                    in_=v_grouped[:].rearrange("p d t -> p (d t)"),
+                )
+
+                qk_ps = psum.tile([P, 2 * S], BF16, tag="tp")
+                for t in range(TILES):
+                    nc.tensor.transpose(qk_ps[:, P * t : P * (t + 1)], q_sb[:, t, head_cols], ident_bf[:])
+                for t in range(TILES):
+                    nc.tensor.transpose(
+                        qk_ps[:, S + P * t : S + P * (t + 1)], k_sb[:, t, head_cols], ident_bf[:]
+                    )
+                qk_t = work.tile([P, 2 * S], BF16)
+                nc.scalar.copy(out=qk_t[:], in_=qk_ps[:])
+
+                neg_max = work.tile([P, TILES], F32)
+                row_sum = work.tile([P, TILES], F32)
+                e_tiles = []
+                for it in range(TILES):
+                    keys = P * (it + 1)
+                    score_ps = psum.tile([P, S], F32, tag="sc")
+                    nc.tensor.matmul(
+                        out=score_ps[:, 0:keys],
+                        lhsT=qk_t[:, P * it : P * (it + 1)],
+                        rhs=qk_t[:, S : S + keys],
+                        start=True,
+                        stop=True,
+                    )
+                    neg_s = stage.tile([P, S], F32)
+                    nc.vector.scalar_tensor_tensor(
+                        out=neg_s[:, 0:keys],
+                        in0=score_ps[:, 0:keys],
+                        scalar=-INV_SQRT_HD,
+                        in1=prior[:, h, S - keys : S],
+                        op0=ALU.mult,
+                        op1=ALU.add,
+                    )
+                    nc.vector.tensor_reduce(
+                        out=neg_max[:, it : it + 1], in_=neg_s[:, 0:keys], axis=AXIS.X, op=ALU.min
+                    )
+                    e_sb = stage.tile([P, S], BF16)
+                    nc.scalar.activation(
+                        out=e_sb[:, 0:keys],
+                        in_=neg_s[:, 0:keys],
+                        func=ACT.Exp,
+                        scale=-1.0,
+                        bias=neg_max[:, it : it + 1],
+                        accum_out=row_sum[:, it : it + 1],
+                    )
+                    e_tiles.append(e_sb)
+
+                grouped_e = e_grouped[h % 2]
+                for pair in range(TILES // 2):
+                    et_ps = psum.tile([P, 2, TILES, P], BF16, tag="et")
+                    for ii in range(2):
+                        it = 2 * pair + ii
+                        for t in range(it + 1):
+                            nc.tensor.transpose(
+                                et_ps[:, ii, t, :], e_tiles[it][:, P * t : P * (t + 1)], ident_bf[:]
+                            )
+                    for ii in range(2):
+                        it = 2 * pair + ii
+                        nc.scalar.copy(
+                            out=grouped_e[:, P * it : P * (it + 1), 0 : it + 1],
+                            in_=et_ps[:, ii, 0 : it + 1, :].rearrange("p t i -> p i t"),
+                        )
+                e_codes = work.tile([P, S], U32, align_bytes=64)
+                e_scales = work.tile([P, S], U8, align_bytes=64)
+                nc.vector.quantize_mx(
+                    out=e_codes[:].bitcast(FP8X4),
+                    scales=e_scales[:],
+                    in_=grouped_e[:].rearrange("p i t -> p (i t)"),
+                )
+
+                o_ps = psum.tile([P, TILES, HD], F32, tag="o", bufs=1)
+                for it in range(TILES):
+                    nc.tensor.matmul_mx(
+                        out=o_ps[:, it, :],
+                        lhsT=e_codes[:, P * it : P * (it + 1)].bitcast(FP8X4),
+                        lhsT_scale=e_scales[:, P * it : P * (it + 1)],
+                        rhs=v_codes[:].bitcast(FP8X4),
+                        rhs_scale=v_scales[:],
+                        start=True,
+                        stop=True,
+                    )
+                inv_sum = work.tile([P, TILES], F32)
+                nc.vector.reciprocal(out=inv_sum[:], in_=row_sum[:])
+                nc.vector.tensor_tensor(
+                    out=out_sb[:, :, head_cols],
+                    in0=o_ps[:],
+                    in1=inv_sum[:].unsqueeze(2).to_broadcast([P, TILES, HD]),
+                    op=ALU.mult,
+                )
+            nc.sync.dma_start(out=out_rows[:, :, cols], in_=out_sb[:])

@@ -23,7 +23,12 @@ K_PASS = P * PACK
 PASSES = D // K_PASS
 TILES = S // P
 GROUP = 4
+GROUPS = H // GROUP
 CHUNK = GROUP * HD
+H8 = 8
+HALVES = H // H8
+COPIES = P // H8
+ROW = 640
 EPS = 1e-5
 INV_SQRT_HD = 1.0 / math.sqrt(HD)
 
@@ -34,249 +39,461 @@ def tile_bayesianattention_pa_kernel(tc, x, wv, q, k, mask, shape, scale, loc, o
     nc = tc.nc
     with ExitStack() as ctx:
         const = ctx.enter_context(tc.tile_pool(name="const", bufs=1))
-        loads = ctx.enter_context(tc.tile_pool(name="loads", bufs=2))
-        stage = ctx.enter_context(tc.tile_pool(name="stage", bufs=4))
+        loads = ctx.enter_context(tc.tile_pool(name="loads", bufs=4))
+        stage = ctx.enter_context(tc.tile_pool(name="stage", bufs=3))
         work = ctx.enter_context(tc.tile_pool(name="work", bufs=2))
-        psum = ctx.enter_context(tc.psum_pool(name="psum", bufs=2))
-
-        ident_bf = const.tile([P, P], BF16)
-        make_identity(nc, ident_bf[:])
-        ident_f32 = const.tile([P, P], F32)
-        make_identity(nc, ident_f32[:])
+        psum = ctx.enter_context(tc.psum_pool(name="psum", bufs=1))
+        ctx.enter_context(tc.manual_schedule())
 
         par_bf = const.tile([P, 3, H], BF16)
-        for row, vec in enumerate((scale, loc, shape)):
+        for n, vec in enumerate((scale, loc, shape)):
             nc.sync.dma_start(
-                out=par_bf[:, row, :],
+                out=par_bf[:, n, :],
                 in_=vec.rearrange("a h b c -> (a h b c)").partition_broadcast(P),
             )
-        mask_diag = const.tile([P, P], BF16)
-        nc.sync.dma_start(out=mask_diag[:], in_=mask[0, 0, 0:P, 0:P])
+        mask_row = const.tile([P, P], BF16)
+        nc.sync.dma_start(out=mask_row[:], in_=mask[0, 0, S - P, S - P : S].partition_broadcast(P))
 
-        exp_loc = const.tile([P, H], F32)
-        exp_neg_loc = const.tile([P, H], F32)
-        eps_h = const.tile([P, H], F32)
-        nc.scalar.activation(out=exp_loc[:], in_=par_bf[:, 1, :], func=ACT.Exp)
-        nc.scalar.activation(out=exp_neg_loc[:], in_=par_bf[:, 1, :], func=ACT.Exp, scale=-1.0)
-        nc.scalar.activation(out=eps_h[:], in_=par_bf[:, 0, :], func=ACT.Exp, scale=-1.0)
-        nc.vector.tensor_scalar_mul(out=eps_h[:], in0=eps_h[:], scalar1=EPS)
-        neg_centre = const.tile([P, H], F32)
-        nc.vector.tensor_sub(out=neg_centre[:], in0=exp_neg_loc[:], in1=exp_loc[:])
-        power = const.tile([P, H], F32)
-        nc.vector.tensor_copy(out=power[:], in_=par_bf[:, 2, :])
-        log_gain = const.tile([P, H], F32)
-        nc.vector.tensor_mul(out=log_gain[:], in0=power[:], in1=par_bf[:, 0, :])
-
-        x_rows = x.rearrange("b (t p) d -> p (b t) d", p=P)
+        x_rows = x.rearrange("b (u p e) d -> p (b u) e d", p=P, e=2)
         x_sb = const.tile([P, TILES, D], BF16)
-        for t in range(TILES):
-            nc.sync.dma_start(out=x_sb[:, t, :], in_=x_rows[:, t, :])
-        x_words = x_sb[:].bitcast(F32)
-        x_codes = const.tile([P, PASSES, S], U32, align_bytes=64)
-        x_scales = const.tile([P, PASSES, S], U8, align_bytes=64)
         for g in range(PASSES):
-            x_grouped = stage.tile([P, S, PACK], BF16, align_bytes=64)
-            grouped_words = x_grouped[:].bitcast(F32)
-            for half in range(2):
-                xt = psum.tile([P, 2, 2 * P], F32, tag="tp")
-                for u in range(2):
-                    first_word = (K_PASS // 2) * g + P * u
-                    for tt in range(2):
-                        nc.tensor.transpose(
-                            xt[:, u, P * tt : P * (tt + 1)],
-                            x_words[:, 2 * half + tt, first_word : first_word + P],
-                            ident_f32[:],
-                        )
-                nc.vector.tensor_copy(
-                    out=grouped_words[:, 2 * P * half : 2 * P * (half + 1), :],
-                    in_=xt[:].rearrange("p u s -> p s u"),
-                )
-            nc.vector.quantize_mx(
-                out=x_codes[:, g, :].bitcast(FP8X4),
-                scales=x_scales[:, g, :],
-                in_=x_grouped[:].rearrange("p s t -> p (s t)"),
-            )
+            feats = slice(K_PASS * g, K_PASS * (g + 1))
+            for u in range(2):
+                nc.sync.dma_start(out=x_sb[:, 2 * u : 2 * u + 2, feats], in_=x_rows[:, u, :, feats])
 
-        dist = const.tile([P, S], F32)
-        nc.gpsimd.iota(
-            dist[:], pattern=[[1, S]], base=-(S - P), channel_multiplier=-1,
-            allow_small_or_imprecise_dtypes=True,
-        )
-        prior = const.tile([P, H, S], F32)
-        for h in range(H):
-            nc.scalar.activation(
-                out=prior[:, h, :], in_=dist[:], func=ACT.Abs, bias=neg_centre[:, h : h + 1]
-            )
-        for h in range(H):
-            nc.scalar.activation(
-                out=prior[:, h, :], in_=prior[:, h, :], func=ACT.Ln, bias=eps_h[:, h : h + 1]
-            )
-        for h in range(H):
-            nc.scalar.activation(
-                out=prior[:, h, :], in_=prior[:, h, :], func=ACT.Exp,
-                scale=power[:, h : h + 1], bias=log_gain[:, h : h + 1],
-            )
-        for c in range(H // GROUP):
-            heads = slice(GROUP * c, GROUP * (c + 1))
-            nc.vector.tensor_tensor(
-                out=prior[:, heads, S - P : S],
-                in0=prior[:, heads, S - P : S],
-                in1=mask_diag[:].unsqueeze(1).to_broadcast([P, GROUP, P]),
-                op=ALU.subtract,
-            )
-
-        e_grouped = [
-            const.tile([P, S, PACK], BF16, align_bytes=64, name="e_grouped%d" % n) for n in range(2)
-        ]
-        for n in range(2):
-            nc.vector.memset(e_grouped[n][:], 0.0)
-
-        wv_rows = wv.rearrange("(r p e) c -> p r e c", p=P, e=2)
+        wv_rows = wv.rearrange("(g p t) c -> p g t c", g=PASSES, t=PACK)
         q_rows = q.rearrange("b (t p) h d -> p (b t) (h d)", p=P)
         k_rows = k.rearrange("b (t p) h d -> p (b t) (h d)", p=P)
         out_rows = out.rearrange("b (t p) c -> p (b t) c", p=P)
+        wv_raw = {}
+        q_sb = {}
+        k_sb = {}
 
-        for c in range(H // GROUP):
+        def load_wv(c):
+            for g in range(PASSES):
+                raw = loads.tile([P, PACK, CHUNK], BF16, name="wv_raw", bufs=8)
+                nc.sync.dma_start(out=raw[:], in_=wv_rows[:, g, :, CHUNK * c : CHUNK * (c + 1)])
+                wv_raw[c, g] = raw
+
+        def load_qk(c):
             cols = slice(CHUNK * c, CHUNK * (c + 1))
-            wv_raw = loads.tile([P, 2 * PASSES, 2, CHUNK], BF16)
-            for e in range(2):
-                nc.sync.dma_start(out=wv_raw[:, :, e, :], in_=wv_rows[:, :, e, cols])
-            q_sb = loads.tile([P, TILES, CHUNK], BF16)
-            nc.sync.dma_start(out=q_sb[:], in_=q_rows[:, :, cols])
-            k_sb = loads.tile([P, TILES, CHUNK], BF16)
-            nc.sync.dma_start(out=k_sb[:], in_=k_rows[:, :, cols])
+            q_tile = loads.tile([P, TILES, CHUNK], BF16, name="q_tile")
+            nc.sync.dma_start(out=q_tile[:], in_=q_rows[:, :, cols])
+            k_tile = loads.tile([P, TILES, CHUNK], BF16, name="k_tile")
+            nc.sync.dma_start(out=k_tile[:], in_=k_rows[:, :, cols])
+            q_sb[c] = q_tile
+            k_sb[c] = k_tile
 
-            wv_codes = work.tile([P, PASSES, CHUNK], U32, align_bytes=64)
-            wv_scales = work.tile([P, PASSES, CHUNK], U8, align_bytes=64)
-            wv_grouped = []
-            for g in range(PASSES):
-                grouped = stage.tile([P, CHUNK, PACK], BF16, align_bytes=64, tag="wv_grouped", name="wv_grouped")
-                four_rows = wv_raw[:, 2 * g : 2 * g + 2, :, :].rearrange("p u e c -> p (u e) c")
-                nc.vector.tensor_copy(
-                    out=grouped[:].rearrange("p (c i) t -> p c t i", i=4),
-                    in_=four_rows.rearrange("p t (c i) -> p c t i", i=4),
+        load_wv(0)
+        load_qk(0)
+
+        ident_f32 = const.tile([P, P], F32)
+        make_identity(nc, ident_f32[:])
+        dist = const.tile([P, ROW], F32)
+        nc.gpsimd.iota(
+            dist[:], pattern=[[-1, ROW]], base=P - 1, channel_multiplier=0,
+            allow_small_or_imprecise_dtypes=True,
+        )
+        ident_bf = const.tile([P, P], BF16)
+        make_identity(nc, ident_bf[:])
+        flip = const.tile([P, P], F32)
+        nc.gpsimd.memset(flip[:], 0.0)
+        nc.gpsimd.affine_select(
+            out=flip[:], in_=flip[:], pattern=[[1, P]], base=-(P - 1), channel_multiplier=1,
+            compare_op=ALU.not_equal, fill=1.0,
+        )
+        warm = const.tile([P, 1], F32)
+        nc.vector.memset(warm[:], 0.0)
+        nc.scalar.activation(out=warm[:], in_=warm[:], func=ACT.Exp)
+        e_rows = [const.tile([P, TILES, S], BF16, name="e_rows%d" % n) for n in range(2)]
+        for n in range(2):
+            for it in (0, 2):
+                nc.vector.memset(e_rows[n][:, it, P * (it + 1) : P * (it + 2)], 0.0)
+        zeros = const.tile([P, P], F32)
+        nc.vector.memset(zeros[:], 0.0)
+        et_low = psum.tile([P, 2, 2, P], F32, tag="et_low")
+        for ii in range(2):
+            nc.tensor.transpose(et_low[:, ii, 1, :], zeros[:], ident_f32[:])
+
+        sel = const.tile([P, H8], F32)
+        nc.vector.tensor_reduce(
+            out=sel[:], in_=ident_f32[:].rearrange("p (a h) -> p h a", h=H8), axis=AXIS.X, op=ALU.add
+        )
+        par_sel = const.tile([P, 3 * HALVES, H8], F32)
+        nc.vector.tensor_tensor(
+            out=par_sel[:],
+            in0=par_bf[:].rearrange("p v (g h) -> p (v g) h", h=H8),
+            in1=sel[:].unsqueeze(1).to_broadcast([P, 3 * HALVES, H8]),
+            op=ALU.mult,
+        )
+        par = const.tile([P, 3 * HALVES], F32)
+        nc.vector.tensor_reduce(out=par[:], in_=par_sel[:], axis=AXIS.X, op=ALU.add)
+        scale_h = par[:, 0:HALVES]
+        loc_h = par[:, HALVES : 2 * HALVES]
+        power = par[:, 2 * HALVES : 3 * HALVES]
+
+        exp_loc = const.tile([P, HALVES], F32)
+        exp_neg_loc = const.tile([P, HALVES], F32)
+        eps_h = const.tile([P, HALVES], F32)
+        nc.scalar.activation(out=exp_neg_loc[:], in_=loc_h, func=ACT.Exp, scale=-1.0)
+        nc.scalar.activation(out=exp_loc[:], in_=loc_h, func=ACT.Exp)
+        nc.scalar.activation(out=eps_h[:], in_=scale_h, func=ACT.Exp, scale=-1.0)
+        neg_centre = const.tile([P, HALVES], F32)
+        nc.vector.tensor_sub(out=neg_centre[:], in0=exp_neg_loc[:], in1=exp_loc[:])
+        nc.vector.tensor_scalar_mul(out=eps_h[:], in0=eps_h[:], scalar1=EPS)
+        log_gain = const.tile([P, HALVES], F32)
+        nc.vector.tensor_mul(out=log_gain[:], in0=power, in1=scale_h)
+
+        row = const.tile([P, HALVES, ROW], F32)
+
+        def prior_rows(g):
+            nc.scalar.activation(out=row[:, g, :], in_=dist[:], func=ACT.Abs, bias=neg_centre[:, g : g + 1])
+            nc.scalar.activation(out=row[:, g, :], in_=row[:, g, :], func=ACT.Ln, bias=eps_h[:, g : g + 1])
+            nc.scalar.activation(
+                out=row[:, g, :], in_=row[:, g, :], func=ACT.Exp,
+                scale=power[:, g : g + 1], bias=log_gain[:, g : g + 1],
+            )
+
+        flat = out.rearrange("b s c -> (b s c)")
+        half_size = P * ROW
+        parked = S * H * HD - HALVES * half_size - 2 * H * HD
+
+        def park(g):
+            nc.vector.tensor_tensor(
+                out=row[:, g, 0:P], in0=row[:, g, 0:P], in1=mask_row[:, ::-1], op=ALU.subtract
+            )
+            nc.vector.tensor_scalar_mul(out=row[:, g, :], in0=row[:, g, :], scalar1=-math.sqrt(HD))
+            first = parked + g * half_size
+            nc.sync.dma_start(
+                out=flat[first : first + half_size].rearrange("(p n) -> p n", p=P), in_=row[:, g, :]
+            )
+
+        prior = const.tile([P, H, S], F32)
+        step = H8 * ROW + H8
+
+        def read_prior(h0, h1):
+            half = h0 // H8
+            heads = slice(h0 % H8, h0 % H8 + h1 - h0)
+            for b in range(H8):
+                first = parked + half * half_size + b
+                nc.sync.dma_start(
+                    out=prior[b:P:H8, h0:h1, :],
+                    in_=flat[first : first + COPIES * step]
+                    .rearrange("(a r) -> a r", a=COPIES)[:, 0 : H8 * ROW]
+                    .rearrange("a (h n) -> a h n", h=H8)[:, heads, 0:S],
                 )
-                wv_grouped.append(grouped)
-            for g in range(PASSES):
-                nc.vector.quantize_mx(
-                    out=wv_codes[:, g, :].bitcast(FP8X4),
-                    scales=wv_scales[:, g, :],
-                    in_=wv_grouped[g][:].rearrange("p c t -> p (c t)"),
-                )
 
-            out_sb = work.tile([P, TILES, CHUNK], F32)
-            for hh in range(GROUP):
-                h = GROUP * c + hh
-                head_cols = slice(HD * hh, HD * (hh + 1))
+        x_words = x_sb[:].bitcast(F32)
+        x_codes = const.tile([P, PASSES, S], U32, align_bytes=64)
+        x_scales = const.tile([P, PASSES, S], U8, align_bytes=64)
 
-                v_ps = psum.tile([P, TILES, HD], F32, tag="v", bufs=1)
-                for t in range(TILES):
-                    for g in range(PASSES):
-                        nc.tensor.matmul_mx(
-                            out=v_ps[:, t, :],
-                            lhsT=x_codes[:, g, P * t : P * (t + 1)].bitcast(FP8X4),
-                            lhsT_scale=x_scales[:, g, P * t : P * (t + 1)],
-                            rhs=wv_codes[:, g, head_cols].bitcast(FP8X4),
-                            rhs_scale=wv_scales[:, g, head_cols],
-                            start=(g == 0),
-                            stop=(g == PASSES - 1),
-                        )
-                v_grouped = work.tile([P, HD, PACK], BF16, align_bytes=64)
-                nc.scalar.copy(out=v_grouped[:], in_=v_ps[:].rearrange("p t d -> p d t"))
-                v_codes = work.tile([P, HD], U32, align_bytes=64)
-                v_scales = work.tile([P, HD], U8, align_bytes=64)
-                nc.vector.quantize_mx(
-                    out=v_codes[:].bitcast(FP8X4),
-                    scales=v_scales[:],
-                    in_=v_grouped[:].rearrange("p d t -> p (d t)"),
-                )
+        def x_transpose(g, half, grouped, copy):
+            xt = psum.tile([P, 2, 2 * P], F32, tag="sc", bufs=3, name="xt")
+            for u in range(2):
+                for tt in range(2):
+                    words = slice((K_PASS // 2) * g + u, (K_PASS // 2) * (g + 1), 2)
+                    nc.tensor.transpose(
+                        xt[:, u, P * tt : P * (tt + 1)], x_words[:, 2 * half + tt, words], ident_f32[:]
+                    )
+            copy(
+                out=grouped[:].bitcast(F32)[:, 2 * P * half : 2 * P * (half + 1), :],
+                in_=xt[:].rearrange("p u s -> p s u"),
+            )
 
-                qk_ps = psum.tile([P, 2 * S], BF16, tag="tp")
-                for t in range(TILES):
-                    nc.tensor.transpose(qk_ps[:, P * t : P * (t + 1)], q_sb[:, t, head_cols], ident_bf[:])
+        def x_quantize(g, grouped):
+            nc.vector.quantize_mx(
+                out=x_codes[:, g, :].bitcast(FP8X4),
+                scales=x_scales[:, g, :],
+                in_=grouped[:].rearrange("p s t -> p (s t)"),
+            )
+
+        wv_codes = {}
+        wv_scales = {}
+        wv_grouped = {}
+
+        def wv_interleave(c, g):
+            grouped = stage.tile([P, CHUNK, PACK], BF16, align_bytes=64, tag="grouped", name="wv_grouped")
+            nc.vector.tensor_copy(
+                out=grouped[:].rearrange("p (c i) t -> p c t i", i=4),
+                in_=wv_raw[c, g][:].rearrange("p t (c i) -> p c t i", i=4),
+            )
+            wv_grouped[c, g] = grouped
+
+        def wv_quantize(c, g):
+            if g == 0:
+                wv_codes[c] = work.tile([P, PASSES, CHUNK], U32, align_bytes=64, name="wv_codes")
+                wv_scales[c] = work.tile([P, PASSES, CHUNK], U8, align_bytes=64, name="wv_scales")
+            nc.vector.quantize_mx(
+                out=wv_codes[c][:, g, :].bitcast(FP8X4),
+                scales=wv_scales[c][:, g, :],
+                in_=wv_grouped[c, g][:].rearrange("p c t -> p (c t)"),
+            )
+
+        qk_ps = {}
+        qk_t = {}
+        v_ps = {}
+        v_grouped = {}
+        v_codes = {}
+        v_scales = {}
+        scores = {}
+        neg_s = {}
+        neg_max = {}
+        row_sum = {}
+        et = {}
+        e_grouped = {}
+        e_codes = {}
+        e_scales = {}
+        o_ps = {}
+        inv_sum = {}
+        out_sb = {}
+
+        def head_cols(h):
+            return slice(HD * (h % GROUP), HD * (h % GROUP + 1))
+
+        def qk_transpose(h):
+            qk_ps[h] = psum.tile([P, 2, S], BF16, tag="qk", name="qk_ps")
+            for n, src in enumerate((q_sb[h // GROUP], k_sb[h // GROUP])):
                 for t in range(TILES):
                     nc.tensor.transpose(
-                        qk_ps[:, S + P * t : S + P * (t + 1)], k_sb[:, t, head_cols], ident_bf[:]
+                        qk_ps[h][:, n, P * t : P * (t + 1)], src[:, t, head_cols(h)], ident_bf[:]
                     )
-                qk_t = work.tile([P, 2 * S], BF16)
-                nc.scalar.copy(out=qk_t[:], in_=qk_ps[:])
 
-                neg_max = work.tile([P, TILES], F32)
-                row_sum = work.tile([P, TILES], F32)
-                e_tiles = []
-                for it in range(TILES):
-                    keys = P * (it + 1)
-                    score_ps = psum.tile([P, S], F32, tag="sc")
-                    nc.tensor.matmul(
-                        out=score_ps[:, 0:keys],
-                        lhsT=qk_t[:, P * it : P * (it + 1)],
-                        rhs=qk_t[:, S : S + keys],
-                        start=True,
-                        stop=True,
-                    )
-                    neg_s = stage.tile([P, S], F32)
-                    nc.vector.scalar_tensor_tensor(
-                        out=neg_s[:, 0:keys],
-                        in0=score_ps[:, 0:keys],
-                        scalar=-INV_SQRT_HD,
-                        in1=prior[:, h, S - keys : S],
-                        op0=ALU.mult,
-                        op1=ALU.add,
-                    )
-                    nc.vector.tensor_reduce(
-                        out=neg_max[:, it : it + 1], in_=neg_s[:, 0:keys], axis=AXIS.X, op=ALU.min
-                    )
-                    e_sb = stage.tile([P, S], BF16)
-                    nc.scalar.activation(
-                        out=e_sb[:, 0:keys],
-                        in_=neg_s[:, 0:keys],
-                        func=ACT.Exp,
-                        scale=-1.0,
-                        bias=neg_max[:, it : it + 1],
-                        accum_out=row_sum[:, it : it + 1],
-                    )
-                    e_tiles.append(e_sb)
+        def qk_copy(h):
+            qk_t[h] = work.tile([P, 2, S], BF16, name="qk_t", bufs=3)
+            nc.scalar.copy(out=qk_t[h][:], in_=qk_ps[h][:])
 
-                grouped_e = e_grouped[h % 2]
-                for pair in range(TILES // 2):
-                    et_ps = psum.tile([P, 2, TILES, P], BF16, tag="et")
-                    for ii in range(2):
-                        it = 2 * pair + ii
-                        for t in range(it + 1):
-                            nc.tensor.transpose(
-                                et_ps[:, ii, t, :], e_tiles[it][:, P * t : P * (t + 1)], ident_bf[:]
-                            )
-                    for ii in range(2):
-                        it = 2 * pair + ii
-                        nc.scalar.copy(
-                            out=grouped_e[:, P * it : P * (it + 1), 0 : it + 1],
-                            in_=et_ps[:, ii, 0 : it + 1, :].rearrange("p t i -> p i t"),
-                        )
-                e_codes = work.tile([P, S], U32, align_bytes=64)
-                e_scales = work.tile([P, S], U8, align_bytes=64)
-                nc.vector.quantize_mx(
-                    out=e_codes[:].bitcast(FP8X4),
-                    scales=e_scales[:],
-                    in_=grouped_e[:].rearrange("p i t -> p (i t)"),
+        def score(h, it):
+            keys = P * (it + 1)
+            ps = psum.tile([P, S], F32, tag="sc", bufs=3, name="score_ps")
+            for t in range(it + 1):
+                nc.tensor.matmul(
+                    out=ps[:, P * t : P * (t + 1)],
+                    lhsT=prior[:, h, P * (it - t) : P * (it - t + 1)],
+                    rhs=flip[:],
+                    is_transpose=True,
+                    start=(t == 0),
+                    stop=False,
+                )
+            nc.tensor.matmul(
+                out=ps[:, 0:keys],
+                lhsT=qk_t[h][:, 0, P * it : P * (it + 1)],
+                rhs=qk_t[h][:, 1, 0:keys],
+                start=False,
+                stop=True,
+            )
+            scores[h, it] = ps
+
+        def least(h, it):
+            keys = P * (it + 1)
+            if it == 0:
+                neg_max[h] = work.tile([P, TILES], F32, name="neg_max")
+            neg_s[h, it] = stage.tile([P, S], F32, name="neg_s", bufs=4)
+            nc.vector.tensor_scalar(
+                out=neg_s[h, it][:, 0:keys],
+                in0=scores[h, it][:, 0:keys],
+                scalar1=-INV_SQRT_HD,
+                scalar2=None,
+                op0=ALU.mult,
+                op1=ALU.min,
+                accum_out=neg_max[h][:, it : it + 1],
+            )
+
+        def exp(h, it):
+            keys = P * (it + 1)
+            if it == 0:
+                row_sum[h] = work.tile([P, TILES], F32, name="row_sum", bufs=4)
+            nc.scalar.activation(
+                out=e_rows[h % 2][:, it, 0:keys],
+                in_=neg_s[h, it][:, 0:keys],
+                func=ACT.Exp,
+                scale=-1.0,
+                bias=neg_max[h][:, it : it + 1],
+                accum_out=row_sum[h][:, it : it + 1],
+            )
+
+        def e_transpose(h, pair):
+            words = e_rows[h % 2][:].rearrange("p t j -> p (t j)").bitcast(F32).rearrange("p (t w) -> p t w", t=TILES)
+            if pair == 0:
+                et[h, pair] = et_low
+            else:
+                et[h, pair] = psum.tile([P, 2, 2, P], F32, tag="et_high", name="et_high")
+            for ii in range(2):
+                for u in range(pair + 1):
+                    nc.tensor.transpose(
+                        et[h, pair][:, ii, u, :], words[:, 2 * pair + ii, P * u : P * (u + 1)], ident_f32[:]
+                    )
+
+        def e_copy(h, pair):
+            if pair == 0:
+                e_grouped[h] = work.tile([P, S, PACK], BF16, align_bytes=64, name="e_grouped")
+            words = e_grouped[h][:].rearrange("p i t -> p (i t)").bitcast(F32).rearrange(
+                "p (n i u) -> p n i u", n=TILES, u=2
+            )
+            nc.scalar.copy(
+                out=words[:, 2 * pair : 2 * pair + 2, :, :],
+                in_=et[h, pair][:].rearrange("p n u i -> p n i u"),
+            )
+
+        def e_quantize(h):
+            e_codes[h] = work.tile([P, S], U32, align_bytes=64, name="e_codes")
+            e_scales[h] = work.tile([P, S], U8, align_bytes=64, name="e_scales")
+            nc.vector.quantize_mx(
+                out=e_codes[h][:].bitcast(FP8X4),
+                scales=e_scales[h][:],
+                in_=e_grouped[h][:].rearrange("p i t -> p (i t)"),
+            )
+
+        def v_matmul(h):
+            c = h // GROUP
+            v_ps[h] = psum.tile([P, TILES, HD], F32, tag="v", name="v_ps")
+            for t in range(TILES):
+                for g in range(PASSES):
+                    nc.tensor.matmul_mx(
+                        out=v_ps[h][:, t, :],
+                        lhsT=x_codes[:, g, P * t : P * (t + 1)].bitcast(FP8X4),
+                        lhsT_scale=x_scales[:, g, P * t : P * (t + 1)],
+                        rhs=wv_codes[c][:, g, head_cols(h)].bitcast(FP8X4),
+                        rhs_scale=wv_scales[c][:, g, head_cols(h)],
+                        start=(g == 0),
+                        stop=(g == PASSES - 1),
+                    )
+
+        def v_copy(h):
+            v_grouped[h] = work.tile([P, HD, PACK], BF16, align_bytes=64, name="v_grouped", bufs=4)
+            nc.scalar.copy(out=v_grouped[h][:], in_=v_ps[h][:].rearrange("p t d -> p d t"))
+
+        def v_quantize(h):
+            v_codes[h] = work.tile([P, HD], U32, align_bytes=64, name="v_codes", bufs=6)
+            v_scales[h] = work.tile([P, HD], U8, align_bytes=64, name="v_scales", bufs=6)
+            nc.vector.quantize_mx(
+                out=v_codes[h][:].bitcast(FP8X4),
+                scales=v_scales[h][:],
+                in_=v_grouped[h][:].rearrange("p d t -> p (d t)"),
+            )
+
+        def weigh(h):
+            o_ps[h] = psum.tile([P, TILES, HD], F32, tag="o", name="o_ps")
+            for it in range(TILES):
+                nc.tensor.matmul_mx(
+                    out=o_ps[h][:, it, :],
+                    lhsT=e_codes[h][:, P * it : P * (it + 1)].bitcast(FP8X4),
+                    lhsT_scale=e_scales[h][:, P * it : P * (it + 1)],
+                    rhs=v_codes[h][:].bitcast(FP8X4),
+                    rhs_scale=v_scales[h][:],
+                    start=True,
+                    stop=True,
                 )
 
-                o_ps = psum.tile([P, TILES, HD], F32, tag="o", bufs=1)
+        def invert(h):
+            inv_sum[h] = work.tile([P, TILES], F32, name="inv_sum")
+            nc.vector.reciprocal(out=inv_sum[h][:], in_=row_sum[h][:])
+
+        def divide(h, on_scalar):
+            c = h // GROUP
+            if h % GROUP == 0:
+                out_sb[c] = work.tile([P, TILES, CHUNK], F32, name="out_sb")
+            if on_scalar:
                 for it in range(TILES):
-                    nc.tensor.matmul_mx(
-                        out=o_ps[:, it, :],
-                        lhsT=e_codes[:, P * it : P * (it + 1)].bitcast(FP8X4),
-                        lhsT_scale=e_scales[:, P * it : P * (it + 1)],
-                        rhs=v_codes[:].bitcast(FP8X4),
-                        rhs_scale=v_scales[:],
-                        start=True,
-                        stop=True,
+                    nc.scalar.activation(
+                        out=out_sb[c][:, it, head_cols(h)], in_=o_ps[h][:, it, :], func=ACT.Copy,
+                        scale=inv_sum[h][:, it : it + 1],
                     )
-                inv_sum = work.tile([P, TILES], F32)
-                nc.vector.reciprocal(out=inv_sum[:], in_=row_sum[:])
+            else:
                 nc.vector.tensor_tensor(
-                    out=out_sb[:, :, head_cols],
-                    in0=o_ps[:],
-                    in1=inv_sum[:].unsqueeze(2).to_broadcast([P, TILES, HD]),
+                    out=out_sb[c][:, :, head_cols(h)],
+                    in0=o_ps[h][:],
+                    in1=inv_sum[h][:].unsqueeze(2).to_broadcast([P, TILES, HD]),
                     op=ALU.mult,
                 )
-            nc.sync.dma_start(out=out_rows[:, :, cols], in_=out_sb[:])
+            if h % GROUP == GROUP - 1:
+                nc.sync.dma_start(out=out_rows[:, :, CHUNK * c : CHUNK * (c + 1)], in_=out_sb[c][:])
+
+        prior_rows(0)
+        x_grouped = {}
+        for g in range(PASSES):
+            x_grouped[g] = stage.tile([P, S, PACK], BF16, align_bytes=64, tag="grouped", name="x_grouped")
+            for half in range(2):
+                x_transpose(g, half, x_grouped[g], nc.vector.tensor_copy)
+            if g > 0:
+                x_quantize(g - 1, x_grouped[g - 1])
+        park(0)
+        read_prior(0, 2)
+        read_prior(2, 4)
+        prior_rows(1)
+        wv_interleave(0, 0)
+        x_quantize(PASSES - 1, x_grouped[PASSES - 1])
+        qk_transpose(0)
+        qk_copy(0)
+        qk_transpose(1)
+        qk_copy(1)
+        load_wv(1)
+        load_qk(1)
+        pieces = [(c, g) for c in range(GROUPS) for g in range(PASSES)]
+        for i in range(1, 4):
+            wv_interleave(*pieces[i])
+            wv_quantize(*pieces[i - 1])
+        park(1)
+        read_prior(4, 8)
+        for c in range(2, GROUPS):
+            read_prior(GROUP * c, GROUP * (c + 1))
+        for c in range(2, GROUPS):
+            load_wv(c)
+            load_qk(c)
+        score(0, 0)
+        score(0, 1)
+
+        for n in range(-0, H + 2):
+            live = 0 <= n < H
+            if n >= 2:
+                invert(n - 2)
+            if live:
+                least(n, 0)
+            if live:
+                exp(n, 0)
+            if 1 <= n <= H:
+                e_transpose(n - 1, 0)
+                e_transpose(n - 1, 1)
+            if 1 <= n <= H:
+                e_copy(n - 1, 0)
+            if 1 <= n <= H:
+                e_copy(n - 1, 1)
+            if live:
+                score(n, 2)
+            if live:
+                least(n, 1)
+            if live:
+                exp(n, 1)
+            if live:
+                score(n, 3)
+            if 0 <= n < H - 2:
+                qk_transpose(n + 2)
+            if 0 <= n and n + 4 - 1 < len(pieces):
+                wv_quantize(*pieces[n + 4 - 1])
+            if 0 <= n and n + 4 < len(pieces):
+                wv_interleave(*pieces[n + 4])
+            if 0 <= n + 0 - 1 < H and n > -0:
+                v_copy(n + 0 - 1)
+            if 0 <= n < H - 2:
+                qk_copy(n + 2)
+            if live:
+                least(n, 2)
+            if live:
+                exp(n, 2)
+            if 1 <= n <= H:
+                e_quantize(n - 1)
+            if live:
+                least(n, 3)
+            if live:
+                exp(n, 3)
+            if 0 <= n + 0 - 1 < H and n > -0:
+                v_quantize(n + 0 - 1)
+            if 0 <= n < H - 1:
+                score(n + 1, 0)
+            if 0 <= n < H - 1:
+                score(n + 1, 1)
+            if n >= 2:
+                weigh(n - 2)
+            if n + 0 < H:
+                v_matmul(n + 0)
+            if n >= 2:
+                divide(n - 2, n < 12 and n % 2 == 0)

@@ -56,8 +56,8 @@ def tile_bayesianattention_pa_kernel(tc, x, wv, q, k, mask, shape, scale, loc, o
 
         x_rows = x.rearrange("b (u p e) d -> p (b u) e d", p=P, e=2)
         x_sb = const.tile([P, TILES, D], BF16)
-        for g in range(PASSES):
-            feats = slice(K_PASS * g, K_PASS * (g + 1))
+        for half in range(2):
+            feats = slice(D // 2 * half, D // 2 * (half + 1))
             for u in range(2):
                 nc.sync.dma_start(out=x_sb[:, 2 * u : 2 * u + 2, feats], in_=x_rows[:, u, :, feats])
 
@@ -71,7 +71,7 @@ def tile_bayesianattention_pa_kernel(tc, x, wv, q, k, mask, shape, scale, loc, o
 
         def load_wv(c):
             for g in range(PASSES):
-                raw = loads.tile([P, PACK, CHUNK], BF16, name="wv_raw", bufs=8)
+                raw = loads.tile([P, PACK, CHUNK], BF16, name="wv_raw", bufs=10)
                 nc.sync.dma_start(out=raw[:], in_=wv_rows[:, g, :, CHUNK * c : CHUNK * (c + 1)])
                 wv_raw[c, g] = raw
 
@@ -405,7 +405,9 @@ def tile_bayesianattention_pa_kernel(tc, x, wv, q, k, mask, shape, scale, loc, o
                     in1=inv_sum[h][:].unsqueeze(2).to_broadcast([P, TILES, HD]),
                     op=ALU.mult,
                 )
-            if h % GROUP == GROUP - 1:
+            if c == GROUPS - 1:
+                nc.sync.dma_start(out=out_rows[:, :, HD * h : HD * (h + 1)], in_=out_sb[c][:, :, head_cols(h)])
+            elif h % GROUP == GROUP - 1:
                 nc.sync.dma_start(out=out_rows[:, :, CHUNK * c : CHUNK * (c + 1)], in_=out_sb[c][:])
 
         prior_rows(0)
@@ -432,17 +434,18 @@ def tile_bayesianattention_pa_kernel(tc, x, wv, q, k, mask, shape, scale, loc, o
         for i in range(1, 4):
             wv_interleave(*pieces[i])
             wv_quantize(*pieces[i - 1])
-        park(1)
         read_prior(4, 8)
-        for c in range(2, GROUPS):
-            read_prior(GROUP * c, GROUP * (c + 1))
-        for c in range(2, GROUPS):
-            load_wv(c)
-            load_qk(c)
+        load_wv(2)
+        load_qk(2)
+        park(1)
+        read_prior(8, 12)
+        read_prior(12, 16)
+        load_wv(3)
+        load_qk(3)
         score(0, 0)
         score(0, 1)
 
-        for n in range(-0, H + 2):
+        for n in range(0, H + 2):
             live = 0 <= n < H
             if n >= 2:
                 invert(n - 2)
@@ -471,8 +474,8 @@ def tile_bayesianattention_pa_kernel(tc, x, wv, q, k, mask, shape, scale, loc, o
                 wv_quantize(*pieces[n + 4 - 1])
             if 0 <= n and n + 4 < len(pieces):
                 wv_interleave(*pieces[n + 4])
-            if 0 <= n + 0 - 1 < H and n > -0:
-                v_copy(n + 0 - 1)
+            if 0 <= n + -1 < H:
+                v_copy(n + -1)
             if 0 <= n < H - 2:
                 qk_copy(n + 2)
             if live:
@@ -485,15 +488,15 @@ def tile_bayesianattention_pa_kernel(tc, x, wv, q, k, mask, shape, scale, loc, o
                 least(n, 3)
             if live:
                 exp(n, 3)
-            if 0 <= n + 0 - 1 < H and n > -0:
-                v_quantize(n + 0 - 1)
+            if 0 <= n + -1 < H:
+                v_quantize(n + -1)
             if 0 <= n < H - 1:
                 score(n + 1, 0)
             if 0 <= n < H - 1:
                 score(n + 1, 1)
             if n >= 2:
                 weigh(n - 2)
-            if n + 0 < H:
+            if 0 <= n + 0 < H:
                 v_matmul(n + 0)
             if n >= 2:
                 divide(n - 2, n < 12 and n % 2 == 0)

@@ -52,7 +52,7 @@ def tile_bayesianattention_pa_kernel(tc, x, wv, q, k, mask, shape, scale, loc, o
                 in_=vec.rearrange("a h b c -> (a h b c)").partition_broadcast(P),
             )
         mask_row = const.tile([P, P], BF16)
-        nc.sync.dma_start(out=mask_row[:], in_=mask[0, 0, S - P, S - P : S].partition_broadcast(P))
+        nc.scalar.dma_start(out=mask_row[:], in_=mask[0, 0, S - P, S - P : S].partition_broadcast(P))
 
         x_rows = x.rearrange("b (u p e) d -> p (b u) e d", p=P, e=2)
         x_sb = const.tile([P, TILES, D], BF16)
@@ -85,7 +85,6 @@ def tile_bayesianattention_pa_kernel(tc, x, wv, q, k, mask, shape, scale, loc, o
             k_sb[c] = k_tile
 
         load_wv(0)
-        load_qk(0)
 
         ident_f32 = const.tile([P, P], F32)
         make_identity(nc, ident_f32[:])
@@ -146,9 +145,13 @@ def tile_bayesianattention_pa_kernel(tc, x, wv, q, k, mask, shape, scale, loc, o
 
         row = const.tile([P, HALVES, ROW], F32)
 
-        def prior_rows(g):
+        def prior_abs(g):
             nc.scalar.activation(out=row[:, g, :], in_=dist[:], func=ACT.Abs, bias=neg_centre[:, g : g + 1])
+
+        def prior_ln(g):
             nc.scalar.activation(out=row[:, g, :], in_=row[:, g, :], func=ACT.Ln, bias=eps_h[:, g : g + 1])
+
+        def prior_exp(g):
             nc.scalar.activation(
                 out=row[:, g, :], in_=row[:, g, :], func=ACT.Exp,
                 scale=power[:, g : g + 1], bias=log_gain[:, g : g + 1],
@@ -174,7 +177,7 @@ def tile_bayesianattention_pa_kernel(tc, x, wv, q, k, mask, shape, scale, loc, o
         def read_prior(h0, h1):
             half = h0 // H8
             heads = slice(h0 % H8, h0 % H8 + h1 - h0)
-            for b in range(H8):
+            for b in (0, 4, 1, 5, 2, 6, 3, 7):
                 first = parked + half * half_size + b
                 nc.sync.dma_start(
                     out=prior[b:P:H8, h0:h1, :],
@@ -343,10 +346,11 @@ def tile_bayesianattention_pa_kernel(tc, x, wv, q, k, mask, shape, scale, loc, o
                 in_=e_grouped[h][:].rearrange("p i t -> p (i t)"),
             )
 
-        def v_matmul(h):
+        def v_matmul(h, tiles):
             c = h // GROUP
-            v_ps[h] = psum.tile([P, TILES, HD], F32, tag="v", name="v_ps")
-            for t in range(TILES):
+            if tiles[0] == 0:
+                v_ps[h] = psum.tile([P, TILES, HD], F32, tag="v", name="v_ps")
+            for t in tiles:
                 for g in range(PASSES):
                     nc.tensor.matmul_mx(
                         out=v_ps[h][:, t, :],
@@ -410,18 +414,23 @@ def tile_bayesianattention_pa_kernel(tc, x, wv, q, k, mask, shape, scale, loc, o
             elif h % GROUP == GROUP - 1:
                 nc.sync.dma_start(out=out_rows[:, :, CHUNK * c : CHUNK * (c + 1)], in_=out_sb[c][:])
 
-        prior_rows(0)
+        prior_abs(0)
+        prior_abs(1)
+        prior_ln(0)
+        prior_ln(1)
+        prior_exp(0)
+        prior_exp(1)
         x_grouped = {}
         for g in range(PASSES):
             x_grouped[g] = stage.tile([P, S, PACK], BF16, align_bytes=64, tag="grouped", name="x_grouped")
             for half in range(2):
-                x_transpose(g, half, x_grouped[g], nc.vector.tensor_copy)
+                x_transpose(g, half, x_grouped[g], nc.scalar.copy if g >= 2 else nc.vector.tensor_copy)
+            if g == 2:
+                park(0)
+                load_qk(0)
+                read_prior(0, 4)
             if g > 0:
                 x_quantize(g - 1, x_grouped[g - 1])
-        park(0)
-        read_prior(0, 2)
-        read_prior(2, 4)
-        prior_rows(1)
         wv_interleave(0, 0)
         x_quantize(PASSES - 1, x_grouped[PASSES - 1])
         qk_transpose(0)
@@ -434,12 +443,11 @@ def tile_bayesianattention_pa_kernel(tc, x, wv, q, k, mask, shape, scale, loc, o
         for i in range(1, 4):
             wv_interleave(*pieces[i])
             wv_quantize(*pieces[i - 1])
+        park(1)
         read_prior(4, 8)
         load_wv(2)
         load_qk(2)
-        park(1)
-        read_prior(8, 12)
-        read_prior(12, 16)
+        read_prior(8, 16)
         load_wv(3)
         load_qk(3)
         score(0, 0)
@@ -497,6 +505,6 @@ def tile_bayesianattention_pa_kernel(tc, x, wv, q, k, mask, shape, scale, loc, o
             if n >= 2:
                 weigh(n - 2)
             if 0 <= n + 0 < H:
-                v_matmul(n + 0)
+                v_matmul(n + 0, (0, 1, 2, 3))
             if n >= 2:
                 divide(n - 2, n < 12 and n % 2 == 0)

from contextlib import ExitStack
import math

import concourse.mybir as mybir
from concourse.masks import make_identity

F32 = mybir.dt.float32
BF16 = mybir.dt.bfloat16
U32 = mybir.dt.uint32
U8 = mybir.dt.uint8
FP8X4 = mybir.dt.float8_e4m3fn_x4
ACT = mybir.ActivationFunctionType
ALU = mybir.AluOpType
AXIS = mybir.AxisListType

P = 128
S = 512
D = 2048
H = 16
HD = 128
PACK = 4
K_PASS = P * PACK
PASSES = D // K_PASS
TILES = S // P
GROUP = 4
GROUPS = H // GROUP
CHUNK = GROUP * HD
H8 = 8
HALVES = H // H8
COPIES = P // H8
ROW = 640
EPS = 1e-5
INV_SQRT_HD = 1.0 / math.sqrt(HD)

FLOPS = 2 * S * D * H * HD + 2 * (2 * H * S * S * HD)


def tile_bayesianattention_pa_kernel(tc, x, wv, q, k, mask, shape, scale, loc, out):
    nc = tc.nc
    with ExitStack() as ctx:
        const = ctx.enter_context(tc.tile_pool(name="const", bufs=1))
        loads = ctx.enter_context(tc.tile_pool(name="loads", bufs=4))
        stage = ctx.enter_context(tc.tile_pool(name="stage", bufs=3))
        work = ctx.enter_context(tc.tile_pool(name="work", bufs=2))
        psum = ctx.enter_context(tc.psum_pool(name="psum", bufs=1))
        ctx.enter_context(tc.manual_schedule())

        par_bf = const.tile([P, 3, H], BF16)
        for n, vec in enumerate((scale, loc, shape)):
            nc.sync.dma_start(
                out=par_bf[:, n, :],
                in_=vec.rearrange("a h b c -> (a h b c)").partition_broadcast(P),
            )
        mask_row = const.tile([P, P], BF16)
        nc.scalar.dma_start(out=mask_row[:], in_=mask[0, 0, S - P, S - P : S].partition_broadcast(P))

        x_rows = x.rearrange("b (u p e) d -> p (b u) e d", p=P, e=2)
        x_sb = const.tile([P, TILES, D], BF16)
        for half in range(2):
            feats = slice(D // 2 * half, D // 2 * (half + 1))
            for u in range(2):
                nc.sync.dma_start(out=x_sb[:, 2 * u : 2 * u + 2, feats], in_=x_rows[:, u, :, feats])

        wv_rows = wv.rearrange("(g p t) c -> p g t c", g=PASSES, t=PACK)
        q_rows = q.rearrange("b (t p) h d -> p (b t) (h d)", p=P)
        k_rows = k.rearrange("b (t p) h d -> p (b t) (h d)", p=P)
        out_rows = out.rearrange("b (t p) c -> p (b t) c", p=P)
        wv_raw = {}
        q_sb = {}
        k_sb = {}

        def load_wv(c):
            for g in range(PASSES):
                raw = loads.tile([P, PACK, CHUNK], BF16, name="wv_raw", bufs=10)
                nc.sync.dma_start(out=raw[:], in_=wv_rows[:, g, :, CHUNK * c : CHUNK * (c + 1)])
                wv_raw[c, g] = raw

        def load_qk(c):
            cols = slice(CHUNK * c, CHUNK * (c + 1))
            q_tile = loads.tile([P, TILES, CHUNK], BF16, name="q_tile")
            nc.sync.dma_start(out=q_tile[:], in_=q_rows[:, :, cols])
            k_tile = loads.tile([P, TILES, CHUNK], BF16, name="k_tile")
            nc.sync.dma_start(out=k_tile[:], in_=k_rows[:, :, cols])
            q_sb[c] = q_tile
            k_sb[c] = k_tile

        load_wv(0)

        ident_f32 = const.tile([P, P], F32)
        make_identity(nc, ident_f32[:])
        dist = const.tile([P, ROW], F32)
        nc.gpsimd.iota(
            dist[:], pattern=[[-1, ROW]], base=P - 1, channel_multiplier=0,
            allow_small_or_imprecise_dtypes=True,
        )
        ident_bf = const.tile([P, P], BF16)
        make_identity(nc, ident_bf[:])
        flip = const.tile([P, P], F32)
        nc.gpsimd.memset(flip[:], 0.0)
        nc.gpsimd.affine_select(
            out=flip[:], in_=flip[:], pattern=[[1, P]], base=-(P - 1), channel_multiplier=1,
            compare_op=ALU.not_equal, fill=1.0,
        )
        warm = const.tile([P, 1], F32)
        nc.vector.memset(warm[:], 0.0)
        nc.scalar.activation(out=warm[:], in_=warm[:], func=ACT.Exp)
        e_rows = [const.tile([P, TILES, S], BF16, name="e_rows%d" % n) for n in range(2)]
        for n in range(2):
            for it in (0, 2):
                nc.vector.memset(e_rows[n][:, it, P * (it + 1) : P * (it + 2)], 0.0)
        zeros = const.tile([P, P], F32)
        nc.vector.memset(zeros[:], 0.0)
        et_low = psum.tile([P, 2, 2, P], F32, tag="et_low")
        for ii in range(2):
            nc.tensor.transpose(et_low[:, ii, 1, :], zeros[:], ident_f32[:])

        sel = const.tile([P, H8], F32)
        nc.vector.tensor_reduce(
            out=sel[:], in_=ident_f32[:].rearrange("p (a h) -> p h a", h=H8), axis=AXIS.X, op=ALU.add
        )
        par_sel = const.tile([P, 3 * HALVES, H8], F32)
        nc.vector.tensor_tensor(
            out=par_sel[:],
            in0=par_bf[:].rearrange("p v (g h) -> p (v g) h", h=H8),
            in1=sel[:].unsqueeze(1).to_broadcast([P, 3 * HALVES, H8]),
            op=ALU.mult,
        )
        par = const.tile([P, 3 * HALVES], F32)
        nc.vector.tensor_reduce(out=par[:], in_=par_sel[:], axis=AXIS.X, op=ALU.add)
        scale_h = par[:, 0:HALVES]
        loc_h = par[:, HALVES : 2 * HALVES]
        power = par[:, 2 * HALVES : 3 * HALVES]

        exp_loc = const.tile([P, HALVES], F32)
        exp_neg_loc = const.tile([P, HALVES], F32)
        eps_h = const.tile([P, HALVES], F32)
        nc.scalar.activation(out=exp_neg_loc[:], in_=loc_h, func=ACT.Exp, scale=-1.0)
        nc.scalar.activation(out=exp_loc[:], in_=loc_h, func=ACT.Exp)
        nc.scalar.activation(out=eps_h[:], in_=scale_h, func=ACT.Exp, scale=-1.0)
        neg_centre = const.tile([P, HALVES], F32)
        nc.vector.tensor_sub(out=neg_centre[:], in0=exp_neg_loc[:], in1=exp_loc[:])
        nc.vector.tensor_scalar_mul(out=eps_h[:], in0=eps_h[:], scalar1=EPS)
        log_gain = const.tile([P, HALVES], F32)
        nc.vector.tensor_mul(out=log_gain[:], in0=power, in1=scale_h)

        row = const.tile([P, HALVES, ROW], F32)

        def prior_abs(g):
            nc.scalar.activation(out=row[:, g, :], in_=dist[:], func=ACT.Abs, bias=neg_centre[:, g : g + 1])

        def prior_ln(g):
            nc.scalar.activation(out=row[:, g, :], in_=row[:, g, :], func=ACT.Ln, bias=eps_h[:, g : g + 1])

        def prior_exp(g):
            nc.scalar.activation(
                out=row[:, g, :], in_=row[:, g, :], func=ACT.Exp,
                scale=power[:, g : g + 1], bias=log_gain[:, g : g + 1],
            )

        flat = out.rearrange("b s c -> (b s c)")
        half_size = P * ROW
        parked = S * H * HD - HALVES * half_size - 2 * H * HD

        def park(g):
            nc.vector.tensor_tensor(
                out=row[:, g, 0:P], in0=row[:, g, 0:P], in1=mask_row[:, ::-1], op=ALU.subtract
            )
            nc.vector.tensor_scalar_mul(out=row[:, g, :], in0=row[:, g, :], scalar1=-math.sqrt(HD))
            first = parked + g * half_size
            nc.sync.dma_start(
                out=flat[first : first + half_size].rearrange("(p n) -> p n", p=P), in_=row[:, g, :]
            )

        prior = const.tile([P, H, S], F32)
        step = H8 * ROW + H8

        def read_prior(h0, h1):
            half = h0 // H8
            heads = slice(h0 % H8, h0 % H8 + h1 - h0)
            for b in (0, 4, 1, 5, 2, 6, 3, 7):
                first = parked + half * half_size + b
                nc.sync.dma_start(
                    out=prior[b:P:H8, h0:h1, :],
                    in_=flat[first : first + COPIES * step]
                    .rearrange("(a r) -> a r", a=COPIES)[:, 0 : H8 * ROW]
                    .rearrange("a (h n) -> a h n", h=H8)[:, heads, 0:S],
                )

        x_words = x_sb[:].bitcast(F32)
        x_codes = const.tile([P, PASSES, S], U32, align_bytes=64)
        x_scales = const.tile([P, PASSES, S], U8, align_bytes=64)

        def x_transpose(g, half, grouped, copy):
            xt = psum.tile([P, 2, 2 * P], F32, tag="sc", bufs=3, name="xt")
            for u in range(2):
                for tt in range(2):
                    words = slice((K_PASS // 2) * g + u, (K_PASS // 2) * (g + 1), 2)
                    nc.tensor.transpose(
                        xt[:, u, P * tt : P * (tt + 1)], x_words[:, 2 * half + tt, words], ident_f32[:]
                    )
            copy(
                out=grouped[:].bitcast(F32)[:, 2 * P * half : 2 * P * (half + 1), :],
                in_=xt[:].rearrange("p u s -> p s u"),
            )

        def x_quantize(g, grouped):
            nc.vector.quantize_mx(
                out=x_codes[:, g, :].bitcast(FP8X4),
                scales=x_scales[:, g, :],
                in_=grouped[:].rearrange("p s t -> p (s t)"),
            )

        wv_codes = {}
        wv_scales = {}
        wv_grouped = {}

        def wv_interleave(c, g):
            grouped = stage.tile([P, CHUNK, PACK], BF16, align_bytes=64, tag="grouped", name="wv_grouped")
            nc.vector.tensor_copy(
                out=grouped[:].rearrange("p (c i) t -> p c t i", i=4),
                in_=wv_raw[c, g][:].rearrange("p t (c i) -> p c t i", i=4),
            )
            wv_grouped[c, g] = grouped

        def wv_quantize(c, g):
            if g == 0:
                wv_codes[c] = work.tile([P, PASSES, CHUNK], U32, align_bytes=64, name="wv_codes")
                wv_scales[c] = work.tile([P, PASSES, CHUNK], U8, align_bytes=64, name="wv_scales")
            nc.vector.quantize_mx(
                out=wv_codes[c][:, g, :].bitcast(FP8X4),
                scales=wv_scales[c][:, g, :],
                in_=wv_grouped[c, g][:].rearrange("p c t -> p (c t)"),
            )

        qk_ps = {}
        qk_t = {}
        v_ps = {}
        v_grouped = {}
        v_codes = {}
        v_scales = {}
        scores = {}
        neg_s = {}
        neg_max = {}
        row_sum = {}
        et = {}
        e_grouped = {}
        e_codes = {}
        e_scales = {}
        o_ps = {}
        inv_sum = {}
        out_sb = {}

        def head_cols(h):
            return slice(HD * (h % GROUP), HD * (h % GROUP + 1))

        def qk_transpose(h):
            qk_ps[h] = psum.tile([P, 2, S], BF16, tag="qk", name="qk_ps")
            for n, src in enumerate((q_sb[h // GROUP], k_sb[h // GROUP])):
                for t in range(TILES):
                    nc.tensor.transpose(
                        qk_ps[h][:, n, P * t : P * (t + 1)], src[:, t, head_cols(h)], ident_bf[:]
                    )

        def qk_copy(h):
            qk_t[h] = work.tile([P, 2, S], BF16, name="qk_t", bufs=3)
            nc.scalar.copy(out=qk_t[h][:], in_=qk_ps[h][:])

        def score(h, it):
            keys = P * (it + 1)
            ps = psum.tile([P, S], F32, tag="sc", bufs=3, name="score_ps")
            for t in range(it + 1):
                nc.tensor.matmul(
                    out=ps[:, P * t : P * (t + 1)],
                    lhsT=prior[:, h, P * (it - t) : P * (it - t + 1)],
                    rhs=flip[:],
                    is_transpose=True,
                    start=(t == 0),
                    stop=False,
                )
            nc.tensor.matmul(
                out=ps[:, 0:keys],
                lhsT=qk_t[h][:, 0, P * it : P * (it + 1)],
                rhs=qk_t[h][:, 1, 0:keys],
                start=False,
                stop=True,
            )
            scores[h, it] = ps

        def least(h, it):
            keys = P * (it + 1)
            if it == 0:
                neg_max[h] = work.tile([P, TILES], F32, name="neg_max")
            neg_s[h, it] = stage.tile([P, S], F32, name="neg_s", bufs=4)
            nc.vector.tensor_scalar(
                out=neg_s[h, it][:, 0:keys],
                in0=scores[h, it][:, 0:keys],
                scalar1=-INV_SQRT_HD,
                scalar2=None,
                op0=ALU.mult,
                op1=ALU.min,
                accum_out=neg_max[h][:, it : it + 1],
            )

        def exp(h, it):
            keys = P * (it + 1)
            if it == 0:
                row_sum[h] = work.tile([P, TILES], F32, name="row_sum", bufs=4)
            nc.scalar.activation(
                out=e_rows[h % 2][:, it, 0:keys],
                in_=neg_s[h, it][:, 0:keys],
                func=ACT.Exp,
                scale=-1.0,
                bias=neg_max[h][:, it : it + 1],
                accum_out=row_sum[h][:, it : it + 1],
            )

        def e_transpose(h, pair):
            words = e_rows[h % 2][:].rearrange("p t j -> p (t j)").bitcast(F32).rearrange("p (t w) -> p t w", t=TILES)
            if pair == 0:
                et[h, pair] = et_low
            else:
                et[h, pair] = psum.tile([P, 2, 2, P], F32, tag="et_high", name="et_high")
            for ii in range(2):
                for u in range(pair + 1):
                    nc.tensor.transpose(
                        et[h, pair][:, ii, u, :], words[:, 2 * pair + ii, P * u : P * (u + 1)], ident_f32[:]
                    )

        def e_copy(h, pair):
            if pair == 0:
                e_grouped[h] = work.tile([P, S, PACK], BF16, align_bytes=64, name="e_grouped")
            words = e_grouped[h][:].rearrange("p i t -> p (i t)").bitcast(F32).rearrange(
                "p (n i u) -> p n i u", n=TILES, u=2
            )
            nc.scalar.copy(
                out=words[:, 2 * pair : 2 * pair + 2, :, :],
                in_=et[h, pair][:].rearrange("p n u i -> p n i u"),
            )

        def e_quantize(h):
            e_codes[h] = work.tile([P, S], U32, align_bytes=64, name="e_codes")
            e_scales[h] = work.tile([P, S], U8, align_bytes=64, name="e_scales")
            nc.vector.quantize_mx(
                out=e_codes[h][:].bitcast(FP8X4),
                scales=e_scales[h][:],
                in_=e_grouped[h][:].rearrange("p i t -> p (i t)"),
            )

        def v_matmul(h, tiles):
            c = h // GROUP
            if tiles[0] == 0:
                v_ps[h] = psum.tile([P, TILES, HD], F32, tag="v", name="v_ps")
            for t in tiles:
                for g in range(PASSES):
                    nc.tensor.matmul_mx(
                        out=v_ps[h][:, t, :],
                        lhsT=x_codes[:, g, P * t : P * (t + 1)].bitcast(FP8X4),
                        lhsT_scale=x_scales[:, g, P * t : P * (t + 1)],
                        rhs=wv_codes[c][:, g, head_cols(h)].bitcast(FP8X4),
                        rhs_scale=wv_scales[c][:, g, head_cols(h)],
                        start=(g == 0),
                        stop=(g == PASSES - 1),
                    )

        def v_copy(h):
            v_grouped[h] = work.tile([P, HD, PACK], BF16, align_bytes=64, name="v_grouped", bufs=4)
            nc.scalar.copy(out=v_grouped[h][:], in_=v_ps[h][:].rearrange("p t d -> p d t"))

        def v_quantize(h):
            v_codes[h] = work.tile([P, HD], U32, align_bytes=64, name="v_codes", bufs=6)
            v_scales[h] = work.tile([P, HD], U8, align_bytes=64, name="v_scales", bufs=6)
            nc.vector.quantize_mx(
                out=v_codes[h][:].bitcast(FP8X4),
                scales=v_scales[h][:],
                in_=v_grouped[h][:].rearrange("p d t -> p (d t)"),
            )

        def weigh(h):
            o_ps[h] = psum.tile([P, TILES, HD], F32, tag="o", name="o_ps")
            for it in range(TILES):
                nc.tensor.matmul_mx(
                    out=o_ps[h][:, it, :],
                    lhsT=e_codes[h][:, P * it : P * (it + 1)].bitcast(FP8X4),
                    lhsT_scale=e_scales[h][:, P * it : P * (it + 1)],
                    rhs=v_codes[h][:].bitcast(FP8X4),
                    rhs_scale=v_scales[h][:],
                    start=True,
                    stop=True,
                )

        def invert(h):
            inv_sum[h] = work.tile([P, TILES], F32, name="inv_sum")
            nc.vector.reciprocal(out=inv_sum[h][:], in_=row_sum[h][:])

        def divide(h, on_scalar):
            c = h // GROUP
            if h % GROUP == 0:
                out_sb[c] = work.tile([P, TILES, CHUNK], F32, name="out_sb")
            if on_scalar:
                for it in range(TILES):
                    nc.scalar.activation(
                        out=out_sb[c][:, it, head_cols(h)], in_=o_ps[h][:, it, :], func=ACT.Copy,
                        scale=inv_sum[h][:, it : it + 1],
                    )
            else:
                nc.vector.tensor_tensor(
                    out=out_sb[c][:, :, head_cols(h)],
                    in0=o_ps[h][:],
                    in1=inv_sum[h][:].unsqueeze(2).to_broadcast([P, TILES, HD]),
                    op=ALU.mult,
                )
            if c == GROUPS - 1:
                nc.sync.dma_start(out=out_rows[:, :, HD * h : HD * (h + 1)], in_=out_sb[c][:, :, head_cols(h)])
            elif h % GROUP == GROUP - 1:
                nc.sync.dma_start(out=out_rows[:, :, CHUNK * c : CHUNK * (c + 1)], in_=out_sb[c][:])

        prior_abs(0)
        prior_abs(1)
        prior_ln(0)
        prior_ln(1)
        prior_exp(0)
        prior_exp(1)
        x_grouped = {}
        for g in range(PASSES):
            x_grouped[g] = stage.tile([P, S, PACK], BF16, align_bytes=64, tag="grouped", name="x_grouped")
            for half in range(2):
                x_transpose(g, half, x_grouped[g], nc.scalar.copy if g >= 2 else nc.vector.tensor_copy)
            if g == 2:
                park(0)
                load_qk(0)
                read_prior(0, 4)
            if g > 0:
                x_quantize(g - 1, x_grouped[g - 1])
        wv_interleave(0, 0)
        x_quantize(PASSES - 1, x_grouped[PASSES - 1])
        qk_transpose(0)
        qk_copy(0)
        qk_transpose(1)
        qk_copy(1)
        load_wv(1)
        load_qk(1)
        pieces = [(c, g) for c in range(GROUPS) for g in range(PASSES)]
        for i in range(1, 4):
            wv_interleave(*pieces[i])
            wv_quantize(*pieces[i - 1])
        park(1)
        read_prior(4, 8)
        load_wv(2)
        load_qk(2)
        read_prior(8, 16)
        load_wv(3)
        load_qk(3)
        score(0, 0)
        score(0, 1)

        for n in range(0, H + 2):
            live = 0 <= n < H
            if n >= 2:
                invert(n - 2)
            if live:
                least(n, 0)
            if live:
                exp(n, 0)
            if 1 <= n <= H:
                e_transpose(n - 1, 0)
                e_transpose(n - 1, 1)
            if 1 <= n <= H:
                e_copy(n - 1, 0)
            if 1 <= n <= H:
                e_copy(n - 1, 1)
            if live:
                score(n, 2)
            if live:
                least(n, 1)
            if live:
                exp(n, 1)
            if live:
                score(n, 3)
            if 0 <= n < H - 2:
                qk_transpose(n + 2)
            if 0 <= n and n + 4 - 1 < len(pieces):
                wv_quantize(*pieces[n + 4 - 1])
            if 0 <= n and n + 4 < len(pieces):
                wv_interleave(*pieces[n + 4])
            if 0 <= n + -1 < H:
                v_copy(n + -1)
            if 0 <= n < H - 2:
                qk_copy(n + 2)
            if live:
                least(n, 2)
            if live:
                exp(n, 2)
            if 1 <= n <= H:
                e_quantize(n - 1)
            if live:
                least(n, 3)
            if live:
                exp(n, 3)
            if 0 <= n + -1 < H:
                v_quantize(n + -1)
            if 0 <= n < H - 1:
                score(n + 1, 0)
            if 0 <= n < H - 1:
                score(n + 1, 1)
            if n >= 2:
                weigh(n - 2)
            if 0 <= n + 0 < H:
                v_matmul(n + 0, (0, 1, 2, 3))
            if n >= 2:
                divide(n - 2, n < 12 and n % 2 == 0)
